import numpy as np
import ml_dtypes


def mxq(x, axis, fmt="e4m3"):
    dtype, down = {"e4m3": (ml_dtypes.float8_e4m3fn, 7), "e5m2": (ml_dtypes.float8_e5m2, 14)}[fmt]
    v = np.moveaxis(np.asarray(x, np.float32).astype(ml_dtypes.bfloat16).astype(np.float64), axis, -1)
    blocks = v.reshape(v.shape[:-1] + (-1, 32))
    amax = np.abs(blocks).max(-1, keepdims=True)
    byte = np.maximum(np.where(amax > 0, np.frexp(amax)[1] - 1 + 127, 0) - down, 1)
    scale = np.exp2(byte - 127.0)
    codes = (blocks / scale).astype(np.float32).astype(dtype).astype(np.float64)
    return np.moveaxis((codes * scale).reshape(v.shape), -1, axis)


WIDE = False


def mx_kscale(k):
    if not WIDE:
        return np.ones(k)
    levels = np.array([10, -10, 5, -5, 0])
    a = np.random.permutation(np.resize(levels, k // 512 * 4)).reshape(k // 512, 4)
    idx = np.arange(k)
    return np.exp2(a[idx // 512, idx % 128 // 32])


BF16 = ml_dtypes.bfloat16


def bf(x):
    return np.asarray(x, np.float32).astype(BF16)


def f64(x):
    return np.asarray(x).astype(np.float64)


E2M1 = np.array([0.0, 0.5, 1.0, 1.5, 2.0, 3.0, 4.0, 6.0, -0.0, -0.5, -1.0, -1.5, -2.0, -3.0, -4.0, -6.0])


def pack_weight(w, fmt):
    k, n = w.shape
    w = f64(bf(w)).reshape(k // 32, 32, n)
    amax = np.abs(w).max(1)
    if fmt == "e4m3":
        byte = np.frexp(amax)[1] - 1 + 127 - 7
    else:
        mant, ex = np.frexp(amax / 6.0)
        byte = np.where(mant > 0.5, ex, ex - 1) + 127
    byte = np.clip(np.where(amax > 0, byte, 1), 1, 254)
    scaled = (w * np.exp2(127.0 - byte)[:, None, :]).reshape(k, n).astype(np.float32)
    by_word = np.ascontiguousarray(scaled.reshape(k // 512, 128, 4, n).transpose(0, 1, 3, 2))
    if fmt == "e4m3":
        words = by_word.astype(ml_dtypes.float8_e4m3fn).view(np.uint8)
    else:
        c = by_word.astype(ml_dtypes.float4_e2m1fn).view(np.uint8) & 0xF
        words = c[..., 0::2] | (c[..., 1::2] << 4)
    return np.ascontiguousarray(words), np.ascontiguousarray(byte.astype(np.uint8).reshape(k // 512, 16, n))


def unpack_weight(words, scales, fmt):
    g, p, n, _ = words.shape
    if fmt == "e4m3":
        vals = np.ascontiguousarray(words).view(ml_dtypes.float8_e4m3fn).astype(np.float64)
    else:
        nib = np.empty((g, p, n, 4), np.uint8)
        nib[..., 0::2] = words & 0xF
        nib[..., 1::2] = words >> 4
        vals = E2M1[nib]
    vals = vals * np.repeat(np.exp2(scales.astype(np.float64) - 127.0), 8, axis=1)[..., None]
    return vals.transpose(0, 1, 3, 2).reshape(g * 512, n)

def pack4(w):
    words, scales = pack_weight(w, "e2m1")
    return words.reshape(words.shape[0], 128, -1), scales


def unpack4(words, scales):
    return unpack_weight(words.reshape(words.shape[0], 128, -1, 2), scales, "e2m1")


B, L, DIM, H, D = 2, 128, 2048, 16, 128
EPS = 1e-6
THETA = 10000.0


def rope_table(seq_len, head_dim):
    pos = np.arange(seq_len, dtype=np.float64)
    inv = 1.0 / (THETA ** (np.arange(0, head_dim, 2, dtype=np.float64) / head_dim))
    ang = pos[:, None] * inv[None, :]
    cos, sin = np.cos(ang), np.sin(ang)
    rot = np.stack([np.stack([cos, -sin], -1), np.stack([sin, cos], -1)], -2)
    return rot[None, None]


def rms_norm(u, gain):
    rrms = 1.0 / np.sqrt(np.mean(np.square(u), axis=-1, keepdims=True) + EPS)
    return u * rrms * gain


def rope(u, table):
    ur = u.reshape(*u.shape[:-1], -1, 1, 2)
    out = table[..., 0] * ur[..., 0] + table[..., 1] * ur[..., 1]
    return out.reshape(u.shape)


def setup_inputs():
    s = mx_kscale(DIM)
    x = bf(np.random.standard_normal((B, L, DIM)) * s)
    pe = bf(rope_table(L, D))
    words, scales = pack4(np.random.standard_normal((DIM, 3 * H * D)) / np.sqrt(DIM) / s[:, None])
    qkv_b = bf(np.random.standard_normal(3 * H * D) * 0.2)
    q_scale = bf(1.0 + 0.1 * np.random.standard_normal(D))
    k_scale = bf(1.0 + 0.1 * np.random.standard_normal(D))
    return {"x": x,
            "pe": pe,
            "qkv_w_words": words,
            "qkv_w_scales": scales,
            "qkv_b": qkv_b,
            "q_scale": q_scale,
            "k_scale": k_scale}


def reference(x, pe, qkv_w_words, qkv_w_scales, qkv_b, q_scale, k_scale):
    qkv = (mxq(f64(x), 2, "e4m3") @ unpack4(qkv_w_words, qkv_w_scales)) + f64(qkv_b)
    qkv = qkv.reshape(B, L, 3, H, D).transpose(2, 0, 3, 1, 4)
    q, k, v = qkv[0], qkv[1], qkv[2]
    q = rms_norm(q, f64(q_scale))
    k = rms_norm(k, f64(k_scale))
    table = f64(pe)
    return rope(q, table), rope(k, table), v

@@ -1,0 +1,285 @@
+from contextlib import ExitStack
+
+import concourse.masks as masks
+import concourse.mybir as mybir
+
+F32 = mybir.dt.float32
+BF16 = mybir.dt.bfloat16
+U8 = mybir.dt.uint8
+U32 = mybir.dt.uint32
+I32 = mybir.dt.int32
+FP8X4 = mybir.dt.float8_e4m3fn_x4
+FP4X4 = mybir.dt.float4_e2m1fn_x4
+ADD = mybir.AluOpType.add
+MULT = mybir.AluOpType.mult
+ACT = mybir.ActivationFunctionType
+
+P = 128
+BATCH = 2
+SEQ = 128
+DIM = 2048
+HEADS = 16
+HEAD_DIM = 128
+PAIRS = HEAD_DIM // 2
+EPS = 1e-6
+K_PASS = 512
+PASSES = DIM // K_PASS
+STREAM_COLS = HEADS * HEAD_DIM
+CHUNK = 512
+CHUNK_HEADS = CHUNK // HEAD_DIM
+CHUNKS_PER_STREAM = STREAM_COLS // CHUNK
+BLOCK = 1024
+CHUNKS_PER_BLOCK = BLOCK // CHUNK
+BLOCKS_PER_STREAM = STREAM_COLS // BLOCK
+
+FLOPS = 2 * BATCH * SEQ * DIM * 3 * STREAM_COLS
+
+
+def tile_selfattention_pa_kernel(
+    tc, x, pe, qkv_w_words, qkv_w_scales, qkv_b, q_scale, k_scale, out_0, out_1, out_2
+):
+    nc = tc.nc
+    outs = [out_0, out_1, out_2]
+    gains = [q_scale, k_scale]
+    words_i32 = qkv_w_words.bitcast(I32)
+    scales_i32 = qkv_w_scales.bitcast(I32)
+
+    with ExitStack() as ctx:
+        ctx.enter_context(tc.manual_schedule())
+        keep = ctx.enter_context(tc.tile_pool(name="keep", bufs=1))
+        work = ctx.enter_context(tc.tile_pool(name="work", bufs=6))
+        stats = ctx.enter_context(tc.tile_pool(name="stats", bufs=6))
+        results = ctx.enter_context(tc.tile_pool(name="results", bufs=12))
+        psum = ctx.enter_context(tc.psum_pool(name="psum", bufs=8))
+
+        x_sb = [keep.tile([P, DIM], BF16, name="x_sb%d" % b) for b in range(BATCH)]
+        x_grouped = [
+            keep.tile([P, PASSES * SEQ * 4], BF16, name="x_grouped%d" % b, align_bytes=64)
+            for b in range(BATCH)
+        ]
+        x_codes = [
+            keep.tile([P, PASSES * SEQ], U32, name="x_codes%d" % b, align_bytes=64)
+            for b in range(BATCH)
+        ]
+        x_scales = [
+            keep.tile([P, PASSES * SEQ], U8, name="x_scales%d" % b, align_bytes=64)
+            for b in range(BATCH)
+        ]
+        w_words = [
+            keep.tile([P, PASSES, 2 * BLOCK], U8, name="w_words%d" % j, align_bytes=64)
+            for j in range(3 * BLOCKS_PER_STREAM)
+        ]
+        w_scales = [
+            keep.tile([P, PASSES, STREAM_COLS], U8, name="w_scales%d" % s, align_bytes=64)
+            for s in range(3)
+        ]
+        bias_sb = keep.tile([P, 3 * STREAM_COLS], BF16, name="bias_sb")
+        pe_sb = keep.tile([P, 4 * PAIRS], BF16, name="pe_sb")
+        gain_sb = [keep.tile([P, HEAD_DIM], BF16, name="gain_sb%d" % s) for s in range(2)]
+        own = [keep.tile([P, HEAD_DIM], F32, name="own%d" % s) for s in range(2)]
+        other = [keep.tile([P, 2, PAIRS], F32, name="other%d" % s) for s in range(2)]
+        ident = keep.tile([P, P], F32, name="ident")
+        table_warm = keep.tile([P, 1], F32, name="table_warm")
+
+        nc.vector.memset(table_warm[:], 1.0)
+        nc.scalar.activation(out=table_warm[:], in_=table_warm[:], func=ACT.Abs_reciprocal_sqrt)
+
+        for b in range(BATCH):
+            nc.sync.dma_start(out=x_sb[b][:], in_=x[b])
+
+        def load_scale_planes(s):
+            nc.vector.memset(w_scales[s][:].bitcast(I32), 0)
+            cols = slice(s * STREAM_COLS // 4, (s + 1) * STREAM_COLS // 4)
+            for first in range(2):
+                for r in range(4):
+                    nc.sync.dma_start(
+                        out=w_scales[s][32 * first + r : P : 64].bitcast(I32),
+                        in_=scales_i32[:, 4 * first + r : 16 : 8, cols].rearrange("g c n -> c g n"),
+                    )
+
+        def load_words(j):
+            cols = slice(j * BLOCK // 2, (j + 1) * BLOCK // 2)
+            nc.sync.dma_start(
+                out=w_words[j][:].bitcast(I32),
+                in_=words_i32[:, :, cols].rearrange("g p c -> p g c"),
+            )
+
+        nc.scalar.dma_start(out=pe_sb[:], in_=pe.rearrange("a b l i e f -> (a b l) (i e f)"))
+        for s in range(2):
+            nc.scalar.dma_start(out=gain_sb[s][:], in_=gains[s].partition_broadcast(P))
+        for s in range(3):
+            load_scale_planes(s)
+            load_words(s * BLOCKS_PER_STREAM)
+            cols = slice(s * STREAM_COLS, (s + 1) * STREAM_COLS)
+            nc.sync.dma_start(out=bias_sb[:, cols], in_=qkv_b[cols].partition_broadcast(P))
+            for j in range(1, BLOCKS_PER_STREAM):
+                load_words(s * BLOCKS_PER_STREAM + j)
+
+        masks.make_identity(nc, ident[:])
+
+        pe_by_pair = pe_sb[:].rearrange("p (i m) -> p i m", m=4)
+        for s in range(2):
+            gain_by_pair = gain_sb[s][:].rearrange("p (i e) -> p i e", e=2)
+            nc.gpsimd.tensor_tensor(
+                out=own[s][:].rearrange("p (i e) -> p i e", e=2),
+                in0=pe_by_pair[:, :, 0:4:3],
+                in1=gain_by_pair,
+                op=MULT,
+            )
+            for e in range(2):
+                nc.gpsimd.tensor_tensor(
+                    out=other[s][:, e, :],
+                    in0=pe_by_pair[:, :, 1 + e],
+                    in1=gain_by_pair[:, :, 1 - e],
+                    op=MULT,
+                )
+
+        def transpose_x(b):
+            words = x_sb[b][:].bitcast(F32)
+            grouped = x_grouped[b][:].bitcast(F32).rearrange(
+                "p (g r u) -> p g r u", g=PASSES, u=2
+            )
+            for half in range(PASSES // 2):
+                xt = psum.tile([P, 4, SEQ], F32, tag="bank", name="xt")
+                for gg in range(2):
+                    g = 2 * half + gg
+                    for u in range(2):
+                        nc.tensor.transpose(
+                            out=xt[:, 2 * gg + u, :],
+                            in_=words[:, 256 * g + u : 256 * (g + 1) : 2],
+                            identity=ident[:],
+                        )
+                source = xt[:].rearrange("p (gg u) r -> p gg r u", u=2)
+                target = grouped[:, 2 * half : 2 * half + 2]
+                if half == 0:
+                    nc.vector.tensor_copy(out=target, in_=source)
+                else:
+                    nc.scalar.copy(out=target, in_=source)
+
+        for b in range(BATCH):
+            transpose_x(b)
+        for b in range(BATCH):
+            nc.vector.quantize_mx(
+                out=x_codes[b][:].bitcast(FP8X4), scales=x_scales[b][:], in_=x_grouped[b][:]
+            )
+
+        steps = [(s, c) for s in range(3) for c in range(CHUNKS_PER_STREAM)]
+
+        def project(s, c, b):
+            block, part = divmod(s * CHUNKS_PER_STREAM + c, CHUNKS_PER_BLOCK)
+            acc = psum.tile([P, CHUNK], F32, tag="bank", name="acc")
+            for g in range(PASSES):
+                tokens = slice(g * SEQ, (g + 1) * SEQ)
+                nc.tensor.matmul_mx(
+                    out=acc[:],
+                    lhsT=x_codes[b][:, tokens].bitcast(FP8X4),
+                    lhsT_scale=x_scales[b][:, tokens],
+                    rhs=w_words[block][:, g, 2 * CHUNK * part : 2 * CHUNK * (part + 1)].bitcast(FP4X4),
+                    rhs_scale=w_scales[s][:, g, CHUNK * c : CHUNK * (c + 1)],
+                    start=(g == 0),
+                    stop=(g == PASSES - 1),
+                )
+            return acc
+
+        def store(s, c, b, res):
+            heads = slice(c * CHUNK_HEADS, (c + 1) * CHUNK_HEADS)
+            nc.sync.dma_start(
+                out=outs[s][b, heads].rearrange("h l d -> l h d"),
+                in_=res[:].rearrange("p (h d) -> p h d", h=CHUNK_HEADS),
+            )
+
+        def add_bias(s, c, pool, name):
+            first_col = s * STREAM_COLS + c * CHUNK
+            accs = [project(s, c, b) for b in range(BATCH)]
+            biased = [pool.tile([P, CHUNK], F32, name=name) for b in range(BATCH)]
+            for b in range(BATCH):
+                nc.vector.tensor_tensor(
+                    out=biased[b][:], in0=accs[b][:],
+                    in1=bias_sb[:, first_col : first_col + CHUNK], op=ADD,
+                )
+            return biased
+
+        def sum_squares(u):
+            squares = work.tile([P, CHUNK], F32, name="squares")
+            sums = stats.tile([P, CHUNK_HEADS], F32, name="sums")
+            for h in range(CHUNK_HEADS):
+                head = slice(h * HEAD_DIM, (h + 1) * HEAD_DIM)
+                nc.scalar.activation(
+                    out=squares[:, head], in_=u[:, head], func=ACT.Square,
+                    accum_out=sums[:, h : h + 1],
+                )
+            return sums
+
+        def reciprocal_rms(sums):
+            rrms = stats.tile([P, CHUNK_HEADS], F32, name="rrms")
+            nc.scalar.activation(
+                out=rrms[:], in_=sums[:], func=ACT.Abs_reciprocal_sqrt,
+                scale=1.0 / HEAD_DIM, bias=EPS,
+            )
+            return rrms
+
+        def partner_product(s, u, from_partner, e):
+            u_by_pair = u[:].rearrange("p (h i e) -> p h i e", h=CHUNK_HEADS, e=2)
+            nc.vector.tensor_tensor(
+                out=from_partner[:, e, :].rearrange("p (h i) -> p h i", h=CHUNK_HEADS),
+                in0=u_by_pair[:, :, :, 1 - e],
+                in1=other[s][:, e, :].unsqueeze(1).to_broadcast([P, CHUNK_HEADS, PAIRS]),
+                op=MULT,
+            )
+
+        def self_product(s, u):
+            from_self = work.tile([P, CHUNK], F32, name="from_self")
+            nc.vector.tensor_tensor(
+                out=from_self[:].rearrange("p (h d) -> p h d", h=CHUNK_HEADS),
+                in0=u[:].rearrange("p (h d) -> p h d", h=CHUNK_HEADS),
+                in1=own[s][:].unsqueeze(1).to_broadcast([P, CHUNK_HEADS, HEAD_DIM]),
+                op=MULT,
+            )
+            return from_self
+
+        def add_products(from_self, from_partner):
+            rotated = work.tile([P, CHUNK], F32, name="rotated")
+            nc.vector.tensor_tensor(
+                out=rotated[:].rearrange("p (c e) -> p c e", e=2),
+                in0=from_self[:].rearrange("p (c e) -> p c e", e=2),
+                in1=from_partner[:].rearrange("p e c -> p c e"),
+                op=ADD,
+            )
+            return rotated
+
+        def normalise(rotated, rrms):
+            res = results.tile([P, CHUNK], F32, name="res")
+            for h in range(CHUNK_HEADS):
+                head = slice(h * HEAD_DIM, (h + 1) * HEAD_DIM)
+                nc.scalar.activation(
+                    out=res[:, head], in_=rotated[:, head], func=ACT.Copy,
+                    scale=rrms[:, h : h + 1],
+                )
+            return res
+
+        batches = range(BATCH)
+        before = None
+        for s, c in steps:
+            if before is not None:
+                s0, c0, u0, rrms0 = before
+                from_partner = [
+                    work.tile([P, 2, CHUNK // 2], F32, name="from_partner") for b in batches
+                ]
+                for e in range(2):
+                    for b in batches:
+                        partner_product(s0, u0[b], from_partner[b], e)
+                from_self = [self_product(s0, u0[b]) for b in batches]
+            if s < 2:
+                u = add_bias(s, c, work, "u")
+                sums = [sum_squares(u[b]) for b in batches]
+            else:
+                v = add_bias(s, c, results, "res")
+                for b in batches:
+                    store(s, c, b, v[b])
+            if before is not None:
+                rotated = [add_products(from_self[b], from_partner[b]) for b in batches]
+                for b in batches:
+                    store(s0, c0, b, normalise(rotated[b], rrms0[b]))
+            before = None
+            if s < 2:
+                before = (s, c, u, [reciprocal_rms(sums[b]) for b in batches])

@@ -28,9 +28,8 @@ STREAM_COLS = HEADS * HEAD_DIM
 CHUNK = 512
 CHUNK_HEADS = CHUNK // HEAD_DIM
 CHUNKS_PER_STREAM = STREAM_COLS // CHUNK
-BLOCK = 1024
-CHUNKS_PER_BLOCK = BLOCK // CHUNK
-BLOCKS_PER_STREAM = STREAM_COLS // BLOCK
+CHUNKS = 3 * CHUNKS_PER_STREAM
+Q, K, V = range(3)
 
 FLOPS = 2 * BATCH * SEQ * DIM * 3 * STREAM_COLS
 
@@ -65,74 +64,95 @@ def tile_selfattention_pa_kernel(
             keep.tile([P, PASSES * SEQ], U8, name="x_scales%d" % b, align_bytes=64)
             for b in range(BATCH)
         ]
+        loads = [(Q, 0, 1), (Q, 1, 1), (Q, 2, 2), (K, 0, 2), (K, 2, 2), (V, 0, 2), (V, 2, 2)]
         w_words = [
-            keep.tile([P, PASSES, 2 * BLOCK], U8, name="w_words%d" % j, align_bytes=64)
-            for j in range(3 * BLOCKS_PER_STREAM)
+            keep.tile([P, PASSES, 2 * CHUNK * n], U8, name="w_words%d_%d" % (s, c), align_bytes=64)
+            for s, c, n in loads
         ]
         w_scales = [
             keep.tile([P, PASSES, STREAM_COLS], U8, name="w_scales%d" % s, align_bytes=64)
-            for s in range(3)
+            for s in (Q, K)
         ]
+        w_scales.append(w_scales[Q])
+        rows = keep.tile([P, CHUNK], BF16, name="rows")
         bias_sb = keep.tile([P, 3 * STREAM_COLS], BF16, name="bias_sb")
         pe_sb = keep.tile([P, 4 * PAIRS], BF16, name="pe_sb")
-        gain_sb = [keep.tile([P, HEAD_DIM], BF16, name="gain_sb%d" % s) for s in range(2)]
-        own = [keep.tile([P, HEAD_DIM], F32, name="own%d" % s) for s in range(2)]
-        other = [keep.tile([P, 2, PAIRS], F32, name="other%d" % s) for s in range(2)]
+        coef = [keep.tile([P, 2, HEAD_DIM], F32, name="coef%d" % s) for s in range(2)]
         ident = keep.tile([P, P], F32, name="ident")
+        ident_bf = keep.tile([P, P], BF16, name="ident_bf")
         table_warm = keep.tile([P, 1], F32, name="table_warm")
 
+        nc.vector.memset(rows[:].bitcast(I32), 0)
         nc.vector.memset(table_warm[:], 1.0)
+        nc.scalar.dma_start(
+            out=rows[0:CHUNKS, :], in_=qkv_b.rearrange("(c n) -> c n", n=CHUNK)
+        )
+        for s in range(2):
+            nc.scalar.dma_start(
+                out=rows[CHUNKS : CHUNKS + 1, s * HEAD_DIM : (s + 1) * HEAD_DIM],
+                in_=gains[s].rearrange("(o n) -> o n", o=1),
+            )
         nc.scalar.activation(out=table_warm[:], in_=table_warm[:], func=ACT.Abs_reciprocal_sqrt)
+        masks.make_identity(nc, ident[:])
+        nc.gpsimd.dma_start(out=pe_sb[:], in_=pe.rearrange("a b l i e f -> (a b l) (i e f)"))
 
-        for b in range(BATCH):
-            nc.sync.dma_start(out=x_sb[b][:], in_=x[b])
+        for s in (Q, K):
+            nc.vector.memset(w_scales[s][:].bitcast(I32), 0)
 
         def load_scale_planes(s):
-            nc.vector.memset(w_scales[s][:].bitcast(I32), 0)
             cols = slice(s * STREAM_COLS // 4, (s + 1) * STREAM_COLS // 4)
-            for first in range(2):
-                for r in range(4):
-                    nc.sync.dma_start(
-                        out=w_scales[s][32 * first + r : P : 64].bitcast(I32),
-                        in_=scales_i32[:, 4 * first + r : 16 : 8, cols].rearrange("g c n -> c g n"),
-                    )
+            for r in range(4):
+                nc.sync.dma_start(
+                    out=w_scales[s][r : P : 32].bitcast(I32),
+                    in_=scales_i32[:, r : 16 : 4, cols].rearrange("g q n -> q g n"),
+                )
 
         def load_words(j):
-            cols = slice(j * BLOCK // 2, (j + 1) * BLOCK // 2)
+            s, c, n = loads[j]
+            first = (s * CHUNKS_PER_STREAM + c) * CHUNK // 2
             nc.sync.dma_start(
                 out=w_words[j][:].bitcast(I32),
-                in_=words_i32[:, :, cols].rearrange("g p c -> p g c"),
+                in_=words_i32[:, :, first : first + n * CHUNK // 2].rearrange("g p c -> p g c"),
             )
 
-        nc.scalar.dma_start(out=pe_sb[:], in_=pe.rearrange("a b l i e f -> (a b l) (i e f)"))
-        for s in range(2):
-            nc.scalar.dma_start(out=gain_sb[s][:], in_=gains[s].partition_broadcast(P))
-        for s in range(3):
-            load_scale_planes(s)
-            load_words(s * BLOCKS_PER_STREAM)
-            cols = slice(s * STREAM_COLS, (s + 1) * STREAM_COLS)
-            nc.sync.dma_start(out=bias_sb[:, cols], in_=qkv_b[cols].partition_broadcast(P))
-            for j in range(1, BLOCKS_PER_STREAM):
-                load_words(s * BLOCKS_PER_STREAM + j)
+        nc.sync.dma_start(out=x_sb[0][:], in_=x[0])
+        load_scale_planes(Q)
+        load_words(0)
+        nc.sync.dma_start(out=x_sb[1][:], in_=x[1])
+        load_words(1)
+        load_words(2)
+        load_scale_planes(K)
+        for j in range(3, len(loads)):
+            load_words(j)
 
-        masks.make_identity(nc, ident[:])
-
-        pe_by_pair = pe_sb[:].rearrange("p (i m) -> p i m", m=4)
-        for s in range(2):
-            gain_by_pair = gain_sb[s][:].rearrange("p (i e) -> p i e", e=2)
-            nc.gpsimd.tensor_tensor(
-                out=own[s][:].rearrange("p (i e) -> p i e", e=2),
-                in0=pe_by_pair[:, :, 0:4:3],
-                in1=gain_by_pair,
-                op=MULT,
+        def spread_row(out, row, width):
+            nc.tensor.matmul(
+                out=out, lhsT=ident_bf[:, row : row + 1].to_broadcast([P, P]),
+                rhs=rows[:, 0:width], start=True, stop=True,
             )
-            for e in range(2):
-                nc.gpsimd.tensor_tensor(
-                    out=other[s][:, e, :],
-                    in0=pe_by_pair[:, :, 1 + e],
-                    in1=gain_by_pair[:, :, 1 - e],
-                    op=MULT,
-                )
+
+        def spread_bias(first):
+            bank = psum.tile([P, 2 * CHUNK], BF16, tag="bank", name="bias_bank")
+            for i in range(2):
+                spread_row(bank[:, i * CHUNK : (i + 1) * CHUNK], first + i, CHUNK)
+            nc.scalar.copy(
+                out=bias_sb[:, first * CHUNK : (first + 2) * CHUNK], in_=bank[:]
+            )
+
+        def make_tables():
+            bank = psum.tile([P, 2 * HEAD_DIM], F32, tag="bank", name="gain_bank")
+            spread_row(bank[:], CHUNKS, 2 * HEAD_DIM)
+            pe_by_pair = pe_sb[:].rearrange("p (i m) -> p i m", m=4)
+            for j, taken in enumerate([slice(0, 4, 3), slice(2, 0, -1)]):
+                for s in range(2):
+                    nc.vector.tensor_tensor(
+                        out=coef[s][:, j, :].rearrange("p (i e) -> p i e", e=2),
+                        in0=pe_by_pair[:, :, taken],
+                        in1=bank[:, s * HEAD_DIM : (s + 1) * HEAD_DIM].rearrange(
+                            "p (i e) -> p i e", e=2
+                        ),
+                        op=MULT,
+                    )
 
         def transpose_x(b):
             words = x_sb[b][:].bitcast(F32)
@@ -156,17 +176,14 @@ def tile_selfattention_pa_kernel(
                 else:
                     nc.scalar.copy(out=target, in_=source)
 
-        for b in range(BATCH):
-            transpose_x(b)
-        for b in range(BATCH):
+        def quantise_x(b):
             nc.vector.quantize_mx(
                 out=x_codes[b][:].bitcast(FP8X4), scales=x_scales[b][:], in_=x_grouped[b][:]
             )
 
-        steps = [(s, c) for s in range(3) for c in range(CHUNKS_PER_STREAM)]
-
         def project(s, c, b):
-            block, part = divmod(s * CHUNKS_PER_STREAM + c, CHUNKS_PER_BLOCK)
+            j = [i for i, (ls, lc, ln) in enumerate(loads) if ls == s and lc <= c < lc + ln][0]
+            part = c - loads[j][1]
             acc = psum.tile([P, CHUNK], F32, tag="bank", name="acc")
             for g in range(PASSES):
                 tokens = slice(g * SEQ, (g + 1) * SEQ)
@@ -174,7 +191,7 @@ def tile_selfattention_pa_kernel(
                     out=acc[:],
                     lhsT=x_codes[b][:, tokens].bitcast(FP8X4),
                     lhsT_scale=x_scales[b][:, tokens],
-                    rhs=w_words[block][:, g, 2 * CHUNK * part : 2 * CHUNK * (part + 1)].bitcast(FP4X4),
+                    rhs=w_words[j][:, g, 2 * CHUNK * part : 2 * CHUNK * (part + 1)].bitcast(FP4X4),
                     rhs_scale=w_scales[s][:, g, CHUNK * c : CHUNK * (c + 1)],
                     start=(g == 0),
                     stop=(g == PASSES - 1),
@@ -188,15 +205,12 @@ def tile_selfattention_pa_kernel(
                 in_=res[:].rearrange("p (h d) -> p h d", h=CHUNK_HEADS),
             )
 
-        def add_bias(s, c, pool, name):
+        def add_bias(s, c, acc, pool, name):
             first_col = s * STREAM_COLS + c * CHUNK
-            accs = [project(s, c, b) for b in range(BATCH)]
-            biased = [pool.tile([P, CHUNK], F32, name=name) for b in range(BATCH)]
-            for b in range(BATCH):
-                nc.vector.tensor_tensor(
-                    out=biased[b][:], in0=accs[b][:],
-                    in1=bias_sb[:, first_col : first_col + CHUNK], op=ADD,
-                )
+            biased = pool.tile([P, CHUNK], F32, name=name)
+            nc.vector.tensor_tensor(
+                out=biased[:], in0=acc[:], in1=bias_sb[:, first_col : first_col + CHUNK], op=ADD
+            )
             return biased
 
         def sum_squares(u):
@@ -218,31 +232,23 @@ def tile_selfattention_pa_kernel(
             )
             return rrms
 
-        def partner_product(s, u, from_partner, e):
-            u_by_pair = u[:].rearrange("p (h i e) -> p h i e", h=CHUNK_HEADS, e=2)
+        def multiply(s, u):
+            products = work.tile([P, 2, CHUNK], F32, name="products")
+            shape = [P, 2, CHUNK_HEADS, HEAD_DIM]
             nc.vector.tensor_tensor(
-                out=from_partner[:, e, :].rearrange("p (h i) -> p h i", h=CHUNK_HEADS),
-                in0=u_by_pair[:, :, :, 1 - e],
-                in1=other[s][:, e, :].unsqueeze(1).to_broadcast([P, CHUNK_HEADS, PAIRS]),
+                out=products[:].rearrange("p j (h d) -> p j h d", h=CHUNK_HEADS),
+                in0=u[:].rearrange("p (h d) -> p h d", h=CHUNK_HEADS).unsqueeze(1).to_broadcast(shape),
+                in1=coef[s][:].unsqueeze(2).to_broadcast(shape),
                 op=MULT,
             )
+            return products
 
-        def self_product(s, u):
-            from_self = work.tile([P, CHUNK], F32, name="from_self")
-            nc.vector.tensor_tensor(
-                out=from_self[:].rearrange("p (h d) -> p h d", h=CHUNK_HEADS),
-                in0=u[:].rearrange("p (h d) -> p h d", h=CHUNK_HEADS),
-                in1=own[s][:].unsqueeze(1).to_broadcast([P, CHUNK_HEADS, HEAD_DIM]),
-                op=MULT,
-            )
-            return from_self
-
-        def add_products(from_self, from_partner):
+        def add_products(products):
             rotated = work.tile([P, CHUNK], F32, name="rotated")
             nc.vector.tensor_tensor(
                 out=rotated[:].rearrange("p (c e) -> p c e", e=2),
-                in0=from_self[:].rearrange("p (c e) -> p c e", e=2),
-                in1=from_partner[:].rearrange("p e c -> p c e"),
+                in0=products[:, 0, :].rearrange("p (c e) -> p c e", e=2),
+                in1=products[:, 1, :].rearrange("p (c e) -> p c e", e=2)[:, :, ::-1],
                 op=ADD,
             )
             return rotated
@@ -257,29 +263,50 @@ def tile_selfattention_pa_kernel(
                 )
             return res
 
-        batches = range(BATCH)
+        steps = [
+            [(Q, 0, 0), (Q, 1, 0)],
+            [(Q, 0, 1), (Q, 1, 1)],
+        ] + [
+            [(s, c, b) for b in range(BATCH)]
+            for s, c in [(Q, 2), (Q, 3), (K, 0), (V, 0), (K, 1), (V, 1), (K, 2), (V, 2), (K, 3), (V, 3)]
+        ]
+
+        nc.vector.tensor_copy(out=ident_bf[:], in_=ident[:])
+        transpose_x(0)
+        quantise_x(0)
+        spread_bias(0)
+        make_tables()
+
         before = None
-        for s, c in steps:
+        for i, step in enumerate(steps):
+            accs = []
+            for j, (s, c, b) in enumerate(step):
+                accs.append(project(s, c, b))
+                if i == 0 and j == 0:
+                    transpose_x(1)
+                    quantise_x(1)
+            if step[0][:2] == (Q, CHUNKS_PER_STREAM - 1):
+                load_scale_planes(V)
+            if 1 <= i < CHUNKS // 2:
+                spread_bias(2 * i)
+            stream = step[0][0]
             if before is not None:
-                s0, c0, u0, rrms0 = before
-                from_partner = [
-                    work.tile([P, 2, CHUNK // 2], F32, name="from_partner") for b in batches
-                ]
-                for e in range(2):
-                    for b in batches:
-                        partner_product(s0, u0[b], from_partner[b], e)
-                from_self = [self_product(s0, u0[b]) for b in batches]
-            if s < 2:
-                u = add_bias(s, c, work, "u")
-                sums = [sum_squares(u[b]) for b in batches]
+                products = [multiply(s, u) for s, c, b, u, rrms in before]
+            if stream == V:
+                if before is not None:
+                    rotated = [add_products(p) for p in products]
+                for (s, c, b), acc in zip(step, accs):
+                    store(s, c, b, add_bias(s, c, acc, results, "res"))
             else:
-                v = add_bias(s, c, results, "res")
-                for b in batches:
-                    store(s, c, b, v[b])
+                us = [add_bias(s, c, acc, work, "u") for (s, c, b), acc in zip(step, accs)]
+                sums = [sum_squares(u) for u in us]
+                if before is not None:
+                    rotated = [add_products(p) for p in products]
             if before is not None:
-                rotated = [add_products(from_self[b], from_partner[b]) for b in batches]
-                for b in batches:
-                    store(s0, c0, b, normalise(rotated[b], rrms0[b]))
+                for (s, c, b, u, rrms), rot in zip(before, rotated):
+                    store(s, c, b, normalise(rot, rrms))
             before = None
-            if s < 2:
-                before = (s, c, u, [reciprocal_rms(sums[b]) for b in batches])
+            if stream != V:
+                before = [
+                    (s, c, b, u, reciprocal_rms(sm)) for (s, c, b), u, sm in zip(step, us, sums)
+                ]

@@ -49,7 +49,8 @@ def tile_selfattention_pa_kernel(
         work = ctx.enter_context(tc.tile_pool(name="work", bufs=6))
         stats = ctx.enter_context(tc.tile_pool(name="stats", bufs=6))
         results = ctx.enter_context(tc.tile_pool(name="results", bufs=12))
-        psum = ctx.enter_context(tc.psum_pool(name="psum", bufs=8))
+        psum = ctx.enter_context(tc.psum_pool(name="psum", bufs=7))
+        psum_keep = ctx.enter_context(tc.psum_pool(name="psum_keep", bufs=1))
 
         x_sb = [keep.tile([P, DIM], BF16, name="x_sb%d" % b) for b in range(BATCH)]
         x_grouped = [
@@ -64,7 +65,7 @@ def tile_selfattention_pa_kernel(
             keep.tile([P, PASSES * SEQ], U8, name="x_scales%d" % b, align_bytes=64)
             for b in range(BATCH)
         ]
-        loads = [(Q, 0, 1), (Q, 1, 1), (Q, 2, 2), (K, 0, 2), (K, 2, 2), (V, 0, 2), (V, 2, 2)]
+        loads = [(Q, 0, 1), (Q, 1, 1), (Q, 2, 2), (K, 0, 2), (V, 0, 2), (K, 2, 2), (V, 2, 2)]
         w_words = [
             keep.tile([P, PASSES, 2 * CHUNK * n], U8, name="w_words%d_%d" % (s, c), align_bytes=64)
             for s, c, n in loads
@@ -77,7 +78,9 @@ def tile_selfattention_pa_kernel(
         rows = keep.tile([P, CHUNK], BF16, name="rows")
         bias_sb = keep.tile([P, 3 * STREAM_COLS], BF16, name="bias_sb")
         pe_sb = keep.tile([P, 4 * PAIRS], BF16, name="pe_sb")
-        coef = [keep.tile([P, 2, HEAD_DIM], F32, name="coef%d" % s) for s in range(2)]
+        coef_sb = keep.tile([P, 2, 2, HEAD_DIM], F32, name="coef_sb")
+        coef_turned = keep.tile([P, 4, P], F32, name="coef_turned")
+        coef = psum_keep.tile([P, 2, 2, HEAD_DIM], F32, name="coef")
         ident = keep.tile([P, P], F32, name="ident")
         ident_bf = keep.tile([P, P], BF16, name="ident_bf")
         table_warm = keep.tile([P, 1], F32, name="table_warm")
@@ -146,13 +149,27 @@ def tile_selfattention_pa_kernel(
             for j, taken in enumerate([slice(0, 4, 3), slice(2, 0, -1)]):
                 for s in range(2):
                     nc.vector.tensor_tensor(
-                        out=coef[s][:, j, :].rearrange("p (i e) -> p i e", e=2),
+                        out=coef_sb[:, s, j, :].rearrange("p (i e) -> p i e", e=2),
                         in0=pe_by_pair[:, :, taken],
                         in1=bank[:, s * HEAD_DIM : (s + 1) * HEAD_DIM].rearrange(
                             "p (i e) -> p i e", e=2
                         ),
                         op=MULT,
                     )
+
+        def turn_tables():
+            bank = psum.tile([P, 4, P], F32, tag="bank", name="turned_bank")
+            tables = coef_sb[:].rearrange("p s j d -> p (s j) d")
+            for t in range(4):
+                nc.tensor.transpose(out=bank[:, t, :], in_=tables[:, t, :], identity=ident[:])
+            nc.scalar.copy(out=coef_turned[:], in_=bank[:])
+
+        def place_tables():
+            tables = coef[:].rearrange("p s j d -> p (s j) d")
+            for t in range(4):
+                nc.tensor.transpose(
+                    out=tables[:, t, :], in_=coef_turned[:, t, :], identity=ident[:]
+                )
 
         def transpose_x(b):
             words = x_sb[b][:].bitcast(F32)
@@ -238,14 +255,14 @@ def tile_selfattention_pa_kernel(
             nc.vector.tensor_tensor(
                 out=products[:].rearrange("p j (h d) -> p j h d", h=CHUNK_HEADS),
                 in0=u[:].rearrange("p (h d) -> p h d", h=CHUNK_HEADS).unsqueeze(1).to_broadcast(shape),
-                in1=coef[s][:].unsqueeze(2).to_broadcast(shape),
+                in1=coef[:, s].unsqueeze(2).to_broadcast(shape),
                 op=MULT,
             )
             return products
 
         def add_products(products):
             rotated = work.tile([P, CHUNK], F32, name="rotated")
-            nc.vector.tensor_tensor(
+            nc.gpsimd.tensor_tensor(
                 out=rotated[:].rearrange("p (c e) -> p c e", e=2),
                 in0=products[:, 0, :].rearrange("p (c e) -> p c e", e=2),
                 in1=products[:, 1, :].rearrange("p (c e) -> p c e", e=2)[:, :, ::-1],
@@ -263,13 +280,14 @@ def tile_selfattention_pa_kernel(
                 )
             return res
 
-        steps = [
-            [(Q, 0, 0), (Q, 1, 0)],
-            [(Q, 0, 1), (Q, 1, 1)],
-        ] + [
-            [(s, c, b) for b in range(BATCH)]
-            for s, c in [(Q, 2), (Q, 3), (K, 0), (V, 0), (K, 1), (V, 1), (K, 2), (V, 2), (K, 3), (V, 3)]
-        ]
+        banks = [(Q, 0, 0), (Q, 1, 0), (Q, 0, 1), (Q, 1, 1)]
+        banks += [(Q, c, b) for c in (2, 3) for b in range(BATCH)]
+        k_banks = [(K, c, b) for c in range(CHUNKS_PER_STREAM) for b in range(BATCH)]
+        v_banks = [(V, c, b) for c in range(CHUNKS_PER_STREAM) for b in range(BATCH)]
+        banks += k_banks[:2]
+        for k_bank, v_bank in zip(k_banks[2:], v_banks):
+            banks += [k_bank, v_bank]
+        banks += v_banks[-2:]
 
         nc.vector.tensor_copy(out=ident_bf[:], in_=ident[:])
         transpose_x(0)
@@ -277,36 +295,30 @@ def tile_selfattention_pa_kernel(
         spread_bias(0)
         make_tables()
 
-        before = None
-        for i, step in enumerate(steps):
-            accs = []
-            for j, (s, c, b) in enumerate(step):
-                accs.append(project(s, c, b))
-                if i == 0 and j == 0:
+        to_rotate, to_normalise = [], []
+        for n in range(len(banks) + 2):
+            rotating, normalising = to_rotate, to_normalise
+            to_rotate, to_normalise = [], []
+            if n < len(banks):
+                s, c, b = banks[n]
+                acc = project(s, c, b)
+                if s == V:
+                    store(s, c, b, add_bias(s, c, acc, results, "res"))
+                else:
+                    u = add_bias(s, c, acc, work, "u")
+                    to_rotate.append((s, c, b, u, sum_squares(u)))
+                if n == 0:
                     transpose_x(1)
                     quantise_x(1)
-            if step[0][:2] == (Q, CHUNKS_PER_STREAM - 1):
-                load_scale_planes(V)
-            if 1 <= i < CHUNKS // 2:
-                spread_bias(2 * i)
-            stream = step[0][0]
-            if before is not None:
-                products = [multiply(s, u) for s, c, b, u, rrms in before]
-            if stream == V:
-                if before is not None:
-                    rotated = [add_products(p) for p in products]
-                for (s, c, b), acc in zip(step, accs):
-                    store(s, c, b, add_bias(s, c, acc, results, "res"))
-            else:
-                us = [add_bias(s, c, acc, work, "u") for (s, c, b), acc in zip(step, accs)]
-                sums = [sum_squares(u) for u in us]
-                if before is not None:
-                    rotated = [add_products(p) for p in products]
-            if before is not None:
-                for (s, c, b, u, rrms), rot in zip(before, rotated):
-                    store(s, c, b, normalise(rot, rrms))
-            before = None
-            if stream != V:
-                before = [
-                    (s, c, b, u, reciprocal_rms(sm)) for (s, c, b), u, sm in zip(step, us, sums)
-                ]
+                    turn_tables()
+                if n == 1:
+                    place_tables()
+                if n % 2 == 1 and n < CHUNKS - 1:
+                    spread_bias(n + 1)
+                if (s, c, b) == (Q, CHUNKS_PER_STREAM - 1, BATCH - 1):
+                    load_scale_planes(V)
+            for s, c, b, u, sums in rotating:
+                rotated = add_products(multiply(s, u))
+                to_normalise.append((s, c, b, rotated, reciprocal_rms(sums)))
+            for s, c, b, rotated, rrms in normalising:
+                store(s, c, b, normalise(rotated, rrms))

@@ -72,10 +72,10 @@ def tile_selfattention_pa_kernel(
         ]
         w_scales = [
             keep.tile([P, PASSES, STREAM_COLS], U8, name="w_scales%d" % s, align_bytes=64)
-            for s in (Q, K)
+            for s in range(3)
         ]
-        w_scales.append(w_scales[Q])
-        rows = keep.tile([P, CHUNK], BF16, name="rows")
+        bias_rows = keep.tile([P, CHUNK], BF16, name="bias_rows")
+        gain_rows = keep.tile([P, 2 * HEAD_DIM], BF16, name="gain_rows")
         bias_sb = keep.tile([P, 3 * STREAM_COLS], BF16, name="bias_sb")
         pe_sb = keep.tile([P, 4 * PAIRS], BF16, name="pe_sb")
         coef_sb = keep.tile([P, 2, 2, HEAD_DIM], F32, name="coef_sb")
@@ -85,28 +85,30 @@ def tile_selfattention_pa_kernel(
         ident_bf = keep.tile([P, P], BF16, name="ident_bf")
         table_warm = keep.tile([P, 1], F32, name="table_warm")
 
-        nc.vector.memset(rows[:].bitcast(I32), 0)
+        nc.vector.memset(bias_rows[:].bitcast(I32), 0)
+        nc.vector.memset(gain_rows[:].bitcast(I32), 0)
         nc.vector.memset(table_warm[:], 1.0)
         nc.scalar.dma_start(
-            out=rows[0:CHUNKS, :], in_=qkv_b.rearrange("(c n) -> c n", n=CHUNK)
+            out=bias_rows[0:CHUNKS, :], in_=qkv_b.rearrange("(c n) -> c n", n=CHUNK)
         )
+        masks.make_identity(nc, ident[:])
         for s in range(2):
             nc.scalar.dma_start(
-                out=rows[CHUNKS : CHUNKS + 1, s * HEAD_DIM : (s + 1) * HEAD_DIM],
+                out=gain_rows[0:1, s * HEAD_DIM : (s + 1) * HEAD_DIM],
                 in_=gains[s].rearrange("(o n) -> o n", o=1),
             )
-        nc.scalar.activation(out=table_warm[:], in_=table_warm[:], func=ACT.Abs_reciprocal_sqrt)
-        masks.make_identity(nc, ident[:])
         nc.gpsimd.dma_start(out=pe_sb[:], in_=pe.rearrange("a b l i e f -> (a b l) (i e f)"))
+        nc.scalar.activation(out=table_warm[:], in_=table_warm[:], func=ACT.Abs_reciprocal_sqrt)
 
-        for s in (Q, K):
-            nc.vector.memset(w_scales[s][:].bitcast(I32), 0)
+        nc.vector.memset(w_scales[Q][:].bitcast(I32), 0)
+        for s in (K, V):
+            nc.gpsimd.memset(w_scales[s][:].bitcast(I32), 0)
 
-        def load_scale_planes(s):
-            cols = slice(s * STREAM_COLS // 4, (s + 1) * STREAM_COLS // 4)
+        def load_scale_planes(s, first, end):
+            cols = slice((s * STREAM_COLS + first) // 4, (s * STREAM_COLS + end) // 4)
             for r in range(4):
                 nc.sync.dma_start(
-                    out=w_scales[s][r : P : 32].bitcast(I32),
+                    out=w_scales[s][r : P : 32, :, first:end].bitcast(I32),
                     in_=scales_i32[:, r : 16 : 4, cols].rearrange("g q n -> q g n"),
                 )
 
@@ -118,33 +120,36 @@ def tile_selfattention_pa_kernel(
                 in_=words_i32[:, :, first : first + n * CHUNK // 2].rearrange("g p c -> p g c"),
             )
 
-        nc.sync.dma_start(out=x_sb[0][:], in_=x[0])
-        load_scale_planes(Q)
+        for b in range(BATCH):
+            nc.sync.dma_start(out=x_sb[b][:], in_=x[b])
+        load_scale_planes(Q, 0, 2 * CHUNK)
         load_words(0)
-        nc.sync.dma_start(out=x_sb[1][:], in_=x[1])
         load_words(1)
+        load_scale_planes(Q, 2 * CHUNK, STREAM_COLS)
         load_words(2)
-        load_scale_planes(K)
-        for j in range(3, len(loads)):
+        load_scale_planes(K, 0, STREAM_COLS)
+        load_words(3)
+        load_scale_planes(V, 0, STREAM_COLS)
+        for j in range(4, len(loads)):
             load_words(j)
 
-        def spread_row(out, row, width):
+        def spread_row(out, rows, row):
             nc.tensor.matmul(
-                out=out, lhsT=ident_bf[:, row : row + 1].to_broadcast([P, P]),
-                rhs=rows[:, 0:width], start=True, stop=True,
+                out=out, lhsT=ident_bf[:, row : row + 1].to_broadcast([P, P]), rhs=rows[:],
+                start=True, stop=True,
             )
 
         def spread_bias(first):
             bank = psum.tile([P, 2 * CHUNK], BF16, tag="bank", name="bias_bank")
             for i in range(2):
-                spread_row(bank[:, i * CHUNK : (i + 1) * CHUNK], first + i, CHUNK)
+                spread_row(bank[:, i * CHUNK : (i + 1) * CHUNK], bias_rows, first + i)
             nc.scalar.copy(
                 out=bias_sb[:, first * CHUNK : (first + 2) * CHUNK], in_=bank[:]
             )
 
         def make_tables():
             bank = psum.tile([P, 2 * HEAD_DIM], F32, tag="bank", name="gain_bank")
-            spread_row(bank[:], CHUNKS, 2 * HEAD_DIM)
+            spread_row(bank[:], gain_rows, 0)
             pe_by_pair = pe_sb[:].rearrange("p (i m) -> p i m", m=4)
             for j, taken in enumerate([slice(0, 4, 3), slice(2, 0, -1)]):
                 for s in range(2):
@@ -280,8 +285,7 @@ def tile_selfattention_pa_kernel(
                 )
             return res
 
-        banks = [(Q, 0, 0), (Q, 1, 0), (Q, 0, 1), (Q, 1, 1)]
-        banks += [(Q, c, b) for c in (2, 3) for b in range(BATCH)]
+        banks = [(Q, c, b) for c in range(CHUNKS_PER_STREAM) for b in range(BATCH)]
         k_banks = [(K, c, b) for c in range(CHUNKS_PER_STREAM) for b in range(BATCH)]
         v_banks = [(V, c, b) for c in range(CHUNKS_PER_STREAM) for b in range(BATCH)]
         banks += k_banks[:2]
@@ -291,9 +295,12 @@ def tile_selfattention_pa_kernel(
 
         nc.vector.tensor_copy(out=ident_bf[:], in_=ident[:])
         transpose_x(0)
-        quantise_x(0)
-        spread_bias(0)
         make_tables()
+        quantise_x(0)
+        transpose_x(1)
+        quantise_x(1)
+        turn_tables()
+        spread_bias(0)
 
         to_rotate, to_normalise = [], []
         for n in range(len(banks) + 2):
@@ -302,21 +309,15 @@ def tile_selfattention_pa_kernel(
             if n < len(banks):
                 s, c, b = banks[n]
                 acc = project(s, c, b)
+                if n == 0:
+                    place_tables()
                 if s == V:
                     store(s, c, b, add_bias(s, c, acc, results, "res"))
                 else:
                     u = add_bias(s, c, acc, work, "u")
                     to_rotate.append((s, c, b, u, sum_squares(u)))
-                if n == 0:
-                    transpose_x(1)
-                    quantise_x(1)
-                    turn_tables()
-                if n == 1:
-                    place_tables()
                 if n % 2 == 1 and n < CHUNKS - 1:
                     spread_bias(n + 1)
-                if (s, c, b) == (Q, CHUNKS_PER_STREAM - 1, BATCH - 1):
-                    load_scale_planes(V)
             for s, c, b, u, sums in rotating:
                 rotated = add_products(multiply(s, u))
                 to_normalise.append((s, c, b, rotated, reciprocal_rms(sums)))

@@ -48,7 +48,7 @@ def tile_selfattention_pa_kernel(
         keep = ctx.enter_context(tc.tile_pool(name="keep", bufs=1))
         work = ctx.enter_context(tc.tile_pool(name="work", bufs=6))
         stats = ctx.enter_context(tc.tile_pool(name="stats", bufs=6))
-        results = ctx.enter_context(tc.tile_pool(name="results", bufs=12))
+        results = ctx.enter_context(tc.tile_pool(name="results", bufs=2 * CHUNKS))
         psum = ctx.enter_context(tc.psum_pool(name="psum", bufs=7))
         psum_keep = ctx.enter_context(tc.psum_pool(name="psum_keep", bufs=1))
 
@@ -70,9 +70,10 @@ def tile_selfattention_pa_kernel(
             keep.tile([P, PASSES, 2 * CHUNK * n], U8, name="w_words%d_%d" % (s, c), align_bytes=64)
             for s, c, n in loads
         ]
+        scale_loads = [(Q, 0, 2), (Q, 2, 2), (K, 0, 4), (V, 0, 4)]
         w_scales = [
-            keep.tile([P, PASSES, STREAM_COLS], U8, name="w_scales%d" % s, align_bytes=64)
-            for s in range(3)
+            keep.tile([P, PASSES, CHUNK * n], U8, name="w_scales%d_%d" % (s, c), align_bytes=64)
+            for s, c, n in scale_loads
         ]
         bias_rows = keep.tile([P, CHUNK], BF16, name="bias_rows")
         gain_rows = keep.tile([P, 2 * HEAD_DIM], BF16, name="gain_rows")
@@ -97,18 +98,19 @@ def tile_selfattention_pa_kernel(
                 out=gain_rows[0:1, s * HEAD_DIM : (s + 1) * HEAD_DIM],
                 in_=gains[s].rearrange("(o n) -> o n", o=1),
             )
-        nc.gpsimd.dma_start(out=pe_sb[:], in_=pe.rearrange("a b l i e f -> (a b l) (i e f)"))
+        nc.scalar.dma_start(out=pe_sb[:], in_=pe.rearrange("a b l i e f -> (a b l) (i e f)"))
         nc.scalar.activation(out=table_warm[:], in_=table_warm[:], func=ACT.Abs_reciprocal_sqrt)
 
-        nc.vector.memset(w_scales[Q][:].bitcast(I32), 0)
-        for s in (K, V):
-            nc.gpsimd.memset(w_scales[s][:].bitcast(I32), 0)
+        for j in range(len(scale_loads)):
+            nc.vector.memset(w_scales[j][:].bitcast(I32), 0)
 
-        def load_scale_planes(s, first, end):
-            cols = slice((s * STREAM_COLS + first) // 4, (s * STREAM_COLS + end) // 4)
+        def load_scale_planes(j):
+            s, c, n = scale_loads[j]
+            first = (s * CHUNKS_PER_STREAM + c) * CHUNK // 4
+            cols = slice(first, first + n * CHUNK // 4)
             for r in range(4):
                 nc.sync.dma_start(
-                    out=w_scales[s][r : P : 32, :, first:end].bitcast(I32),
+                    out=w_scales[j][r : P : 32].bitcast(I32),
                     in_=scales_i32[:, r : 16 : 4, cols].rearrange("g q n -> q g n"),
                 )
 
@@ -122,14 +124,14 @@ def tile_selfattention_pa_kernel(
 
         for b in range(BATCH):
             nc.sync.dma_start(out=x_sb[b][:], in_=x[b])
-        load_scale_planes(Q, 0, 2 * CHUNK)
+        load_scale_planes(0)
         load_words(0)
         load_words(1)
-        load_scale_planes(Q, 2 * CHUNK, STREAM_COLS)
+        load_scale_planes(1)
         load_words(2)
-        load_scale_planes(K, 0, STREAM_COLS)
+        load_scale_planes(2)
         load_words(3)
-        load_scale_planes(V, 0, STREAM_COLS)
+        load_scale_planes(3)
         for j in range(4, len(loads)):
             load_words(j)
 
@@ -203,9 +205,14 @@ def tile_selfattention_pa_kernel(
                 out=x_codes[b][:].bitcast(FP8X4), scales=x_scales[b][:], in_=x_grouped[b][:]
             )
 
+        def place(table, s, c):
+            for j, (ls, first, n) in enumerate(table):
+                if ls == s and first <= c < first + n:
+                    return j, c - first
+
         def project(s, c, b):
-            j = [i for i, (ls, lc, ln) in enumerate(loads) if ls == s and lc <= c < lc + ln][0]
-            part = c - loads[j][1]
+            j, part = place(loads, s, c)
+            sj, spart = place(scale_loads, s, c)
             acc = psum.tile([P, CHUNK], F32, tag="bank", name="acc")
             for g in range(PASSES):
                 tokens = slice(g * SEQ, (g + 1) * SEQ)
@@ -214,7 +221,7 @@ def tile_selfattention_pa_kernel(
                     lhsT=x_codes[b][:, tokens].bitcast(FP8X4),
                     lhsT_scale=x_scales[b][:, tokens],
                     rhs=w_words[j][:, g, 2 * CHUNK * part : 2 * CHUNK * (part + 1)].bitcast(FP4X4),
-                    rhs_scale=w_scales[s][:, g, CHUNK * c : CHUNK * (c + 1)],
+                    rhs_scale=w_scales[sj][:, g, CHUNK * spart : CHUNK * (spart + 1)],
                     start=(g == 0),
                     stop=(g == PASSES - 1),
                 )

@@ -17,6 +17,7 @@ ACT = mybir.ActivationFunctionType
 P = 128
 BATCH = 2
 SEQ = 128
+TOKEN_TILES = 2
 DIM = 2048
 HEADS = 16
 HEAD_DIM = 128
@@ -48,21 +49,21 @@ def tile_selfattention_pa_kernel(
         keep = ctx.enter_context(tc.tile_pool(name="keep", bufs=1))
         work = ctx.enter_context(tc.tile_pool(name="work", bufs=6))
         stats = ctx.enter_context(tc.tile_pool(name="stats", bufs=6))
-        results = ctx.enter_context(tc.tile_pool(name="results", bufs=2 * CHUNKS))
-        psum = ctx.enter_context(tc.psum_pool(name="psum", bufs=7))
+        results = ctx.enter_context(tc.tile_pool(name="results", bufs=CHUNKS))
+        psum = ctx.enter_context(tc.psum_pool(name="psum", bufs=6))
         psum_keep = ctx.enter_context(tc.psum_pool(name="psum_keep", bufs=1))
 
-        x_sb = [keep.tile([P, DIM], BF16, name="x_sb%d" % b) for b in range(BATCH)]
+        x_sb = [keep.tile([P, DIM], BF16, name="x_sb%d" % b) for b in range(TOKEN_TILES)]
         x_grouped = [
-            keep.tile([P, PASSES * SEQ * 4], BF16, name="x_grouped%d" % b, align_bytes=64)
+            keep.tile([P, PASSES * P * 4], BF16, name="x_grouped%d" % b, align_bytes=64)
             for b in range(BATCH)
         ]
         x_codes = [
-            keep.tile([P, PASSES * SEQ], U32, name="x_codes%d" % b, align_bytes=64)
+            keep.tile([P, PASSES * P], U32, name="x_codes%d" % b, align_bytes=64)
             for b in range(BATCH)
         ]
         x_scales = [
-            keep.tile([P, PASSES * SEQ], U8, name="x_scales%d" % b, align_bytes=64)
+            keep.tile([P, PASSES * P], U8, name="x_scales%d" % b, align_bytes=64)
             for b in range(BATCH)
         ]
         loads = [(Q, 0, 1), (Q, 1, 1), (Q, 2, 2), (K, 0, 2), (V, 0, 2), (K, 2, 2), (V, 2, 2)]
@@ -78,10 +79,12 @@ def tile_selfattention_pa_kernel(
         bias_rows = keep.tile([P, CHUNK], BF16, name="bias_rows")
         gain_rows = keep.tile([P, 2 * HEAD_DIM], BF16, name="gain_rows")
         bias_sb = keep.tile([P, 3 * STREAM_COLS], BF16, name="bias_sb")
-        pe_sb = keep.tile([P, 4 * PAIRS], BF16, name="pe_sb")
-        coef_sb = keep.tile([P, 2, 2, HEAD_DIM], F32, name="coef_sb")
-        coef_turned = keep.tile([P, 4, P], F32, name="coef_turned")
-        coef = psum_keep.tile([P, 2, 2, HEAD_DIM], F32, name="coef")
+        pe_sb = keep.tile([P, TOKEN_TILES, 4 * PAIRS], BF16, name="pe_sb")
+        coef_sb = keep.tile([P, 2, TOKEN_TILES, 2, HEAD_DIM], F32, name="coef_sb")
+        coef_turned = [keep.tile([P, 4, P], F32, name="coef_turned%d" % s) for s in range(2)]
+        coef = [
+            psum_keep.tile([P, TOKEN_TILES, 2, HEAD_DIM], F32, name="coef%d" % s) for s in range(2)
+        ]
         ident = keep.tile([P, P], F32, name="ident")
         ident_bf = keep.tile([P, P], BF16, name="ident_bf")
         table_warm = keep.tile([P, 1], F32, name="table_warm")
@@ -98,7 +101,11 @@ def tile_selfattention_pa_kernel(
                 out=gain_rows[0:1, s * HEAD_DIM : (s + 1) * HEAD_DIM],
                 in_=gains[s].rearrange("(o n) -> o n", o=1),
             )
-        nc.scalar.dma_start(out=pe_sb[:], in_=pe.rearrange("a b l i e f -> (a b l) (i e f)"))
+        for b in range(BATCH):
+            nc.scalar.dma_start(
+                out=pe_sb[b:P:BATCH].rearrange("p t m -> p (t m)"),
+                in_=pe.rearrange("a b (j t) i e f -> (a b j) (t i e f)", t=TOKEN_TILES),
+            )
         nc.scalar.activation(out=table_warm[:], in_=table_warm[:], func=ACT.Abs_reciprocal_sqrt)
 
         for j in range(len(scale_loads)):
@@ -122,8 +129,12 @@ def tile_selfattention_pa_kernel(
                 in_=words_i32[:, :, first : first + n * CHUNK // 2].rearrange("g p c -> p g c"),
             )
 
-        for b in range(BATCH):
-            nc.sync.dma_start(out=x_sb[b][:], in_=x[b])
+        for t in range(TOKEN_TILES):
+            for b in range(BATCH):
+                nc.sync.dma_start(
+                    out=x_sb[t][b:P:BATCH],
+                    in_=x[b].rearrange("(j t) k -> t j k", t=TOKEN_TILES)[t],
+                )
         load_scale_planes(0)
         load_words(0)
         load_words(1)
@@ -152,30 +163,31 @@ def tile_selfattention_pa_kernel(
         def make_tables():
             bank = psum.tile([P, 2 * HEAD_DIM], F32, tag="bank", name="gain_bank")
             spread_row(bank[:], gain_rows, 0)
-            pe_by_pair = pe_sb[:].rearrange("p (i m) -> p i m", m=4)
+            pe_by_pair = pe_sb[:].rearrange("p t (i m) -> p t i m", m=4)
             for j, taken in enumerate([slice(0, 4, 3), slice(2, 0, -1)]):
                 for s in range(2):
+                    gain = bank[:, s * HEAD_DIM : (s + 1) * HEAD_DIM]
                     nc.vector.tensor_tensor(
-                        out=coef_sb[:, s, j, :].rearrange("p (i e) -> p i e", e=2),
-                        in0=pe_by_pair[:, :, taken],
-                        in1=bank[:, s * HEAD_DIM : (s + 1) * HEAD_DIM].rearrange(
-                            "p (i e) -> p i e", e=2
-                        ),
+                        out=coef_sb[:, s, :, j, :].rearrange("p t (i e) -> p t i e", e=2),
+                        in0=pe_by_pair[:, :, :, taken],
+                        in1=gain.rearrange("p (i e) -> p i e", e=2)
+                        .unsqueeze(1)
+                        .to_broadcast([P, TOKEN_TILES, PAIRS, 2]),
                         op=MULT,
                     )
 
-        def turn_tables():
+        def turn_tables(s):
             bank = psum.tile([P, 4, P], F32, tag="bank", name="turned_bank")
-            tables = coef_sb[:].rearrange("p s j d -> p (s j) d")
-            for t in range(4):
-                nc.tensor.transpose(out=bank[:, t, :], in_=tables[:, t, :], identity=ident[:])
-            nc.scalar.copy(out=coef_turned[:], in_=bank[:])
+            tables = coef_sb[:, s].rearrange("p t j d -> p (t j) d")
+            for i in range(4):
+                nc.tensor.transpose(out=bank[:, i, :], in_=tables[:, i, :], identity=ident[:])
+            nc.scalar.copy(out=coef_turned[s][:], in_=bank[:])
 
-        def place_tables():
-            tables = coef[:].rearrange("p s j d -> p (s j) d")
-            for t in range(4):
+        def place_tables(s):
+            tables = coef[s][:].rearrange("p t j d -> p (t j) d")
+            for i in range(4):
                 nc.tensor.transpose(
-                    out=tables[:, t, :], in_=coef_turned[:, t, :], identity=ident[:]
+                    out=tables[:, i, :], in_=coef_turned[s][:, i, :], identity=ident[:]
                 )
 
         def transpose_x(b):
@@ -184,7 +196,7 @@ def tile_selfattention_pa_kernel(
                 "p (g r u) -> p g r u", g=PASSES, u=2
             )
             for half in range(PASSES // 2):
-                xt = psum.tile([P, 4, SEQ], F32, tag="bank", name="xt")
+                xt = psum.tile([P, 4, P], F32, tag="bank", name="xt")
                 for gg in range(2):
                     g = 2 * half + gg
                     for u in range(2):
@@ -205,17 +217,17 @@ def tile_selfattention_pa_kernel(
                 out=x_codes[b][:].bitcast(FP8X4), scales=x_scales[b][:], in_=x_grouped[b][:]
             )
 
-        def place(table, s, c):
+        def find_load(table, s, c):
             for j, (ls, first, n) in enumerate(table):
                 if ls == s and first <= c < first + n:
                     return j, c - first
 
         def project(s, c, b):
-            j, part = place(loads, s, c)
-            sj, spart = place(scale_loads, s, c)
+            j, part = find_load(loads, s, c)
+            sj, spart = find_load(scale_loads, s, c)
             acc = psum.tile([P, CHUNK], F32, tag="bank", name="acc")
             for g in range(PASSES):
-                tokens = slice(g * SEQ, (g + 1) * SEQ)
+                tokens = slice(g * P, (g + 1) * P)
                 nc.tensor.matmul_mx(
                     out=acc[:],
                     lhsT=x_codes[b][:, tokens].bitcast(FP8X4),
@@ -227,20 +239,35 @@ def tile_selfattention_pa_kernel(
                 )
             return acc
 
-        def store(s, c, b, res):
-            heads = slice(c * CHUNK_HEADS, (c + 1) * CHUNK_HEADS)
-            nc.sync.dma_start(
-                out=outs[s][b, heads].rearrange("h l d -> l h d"),
-                in_=res[:].rearrange("p (h d) -> p h d", h=CHUNK_HEADS),
-            )
+        chunk_results = {}
 
-        def add_bias(s, c, acc, pool, name):
+        def result_of(s, c):
+            if (s, c) not in chunk_results:
+                chunk_results[s, c] = results.tile(
+                    [P, CHUNK_HEADS, TOKEN_TILES, HEAD_DIM], F32, name="res"
+                )
+            return chunk_results[s, c]
+
+        def store(s, c, t):
+            if t == 0:
+                return
+            heads = slice(c * CHUNK_HEADS, (c + 1) * CHUNK_HEADS)
+            res = result_of(s, c)
+            for b in range(BATCH):
+                nc.sync.dma_start(
+                    out=outs[s][b, heads].rearrange("h (j t) d -> j h (t d)", t=TOKEN_TILES),
+                    in_=res[b:P:BATCH].rearrange("p h t d -> p h (t d)"),
+                )
+
+        def add_bias(s, c, acc, out):
             first_col = s * STREAM_COLS + c * CHUNK
-            biased = pool.tile([P, CHUNK], F32, name=name)
+            bias = bias_sb[:, first_col : first_col + CHUNK]
             nc.vector.tensor_tensor(
-                out=biased[:], in0=acc[:], in1=bias_sb[:, first_col : first_col + CHUNK], op=ADD
+                out=out,
+                in0=acc[:].rearrange("p (h d) -> p h d", h=CHUNK_HEADS),
+                in1=bias.rearrange("p (h d) -> p h d", h=CHUNK_HEADS),
+                op=ADD,
             )
-            return biased
 
         def sum_squares(u):
             squares = work.tile([P, CHUNK], F32, name="squares")
@@ -261,13 +288,13 @@ def tile_selfattention_pa_kernel(
             )
             return rrms
 
-        def multiply(s, u):
+        def multiply(s, t, u):
             products = work.tile([P, 2, CHUNK], F32, name="products")
             shape = [P, 2, CHUNK_HEADS, HEAD_DIM]
             nc.vector.tensor_tensor(
                 out=products[:].rearrange("p j (h d) -> p j h d", h=CHUNK_HEADS),
                 in0=u[:].rearrange("p (h d) -> p h d", h=CHUNK_HEADS).unsqueeze(1).to_broadcast(shape),
-                in1=coef[:, s].unsqueeze(2).to_broadcast(shape),
+                in1=coef[s][:, t].unsqueeze(2).to_broadcast(shape),
                 op=MULT,
             )
             return products
@@ -282,15 +309,13 @@ def tile_selfattention_pa_kernel(
             )
             return rotated
 
-        def normalise(rotated, rrms):
-            res = results.tile([P, CHUNK], F32, name="res")
+        def normalise(rotated, rrms, out):
             for h in range(CHUNK_HEADS):
                 head = slice(h * HEAD_DIM, (h + 1) * HEAD_DIM)
                 nc.scalar.activation(
-                    out=res[:, head], in_=rotated[:, head], func=ACT.Copy,
+                    out=out[:, h, :], in_=rotated[:, head], func=ACT.Copy,
                     scale=rrms[:, h : h + 1],
                 )
-            return res
 
         banks = [(Q, c, b) for c in range(CHUNKS_PER_STREAM) for b in range(BATCH)]
         k_banks = [(K, c, b) for c in range(CHUNKS_PER_STREAM) for b in range(BATCH)]
@@ -306,7 +331,7 @@ def tile_selfattention_pa_kernel(
         quantise_x(0)
         transpose_x(1)
         quantise_x(1)
-        turn_tables()
+        turn_tables(Q)
         spread_bias(0)
 
         to_rotate, to_normalise = [], []
@@ -317,16 +342,23 @@ def tile_selfattention_pa_kernel(
                 s, c, b = banks[n]
                 acc = project(s, c, b)
                 if n == 0:
-                    place_tables()
+                    place_tables(Q)
+                if n == 2:
+                    turn_tables(K)
+                if n == 4:
+                    place_tables(K)
                 if s == V:
-                    store(s, c, b, add_bias(s, c, acc, results, "res"))
+                    add_bias(s, c, acc, result_of(s, c)[:, :, b, :])
+                    store(s, c, b)
                 else:
-                    u = add_bias(s, c, acc, work, "u")
+                    u = work.tile([P, CHUNK], F32, name="u")
+                    add_bias(s, c, acc, u[:].rearrange("p (h d) -> p h d", h=CHUNK_HEADS))
                     to_rotate.append((s, c, b, u, sum_squares(u)))
                 if n % 2 == 1 and n < CHUNKS - 1:
                     spread_bias(n + 1)
             for s, c, b, u, sums in rotating:
-                rotated = add_products(multiply(s, u))
+                rotated = add_products(multiply(s, b, u))
                 to_normalise.append((s, c, b, rotated, reciprocal_rms(sums)))
             for s, c, b, rotated, rrms in normalising:
-                store(s, c, b, normalise(rotated, rrms))
+                normalise(rotated, rrms, result_of(s, c)[:, :, b, :])
+                store(s, c, b)

@@ -31,6 +31,7 @@ CHUNK_HEADS = CHUNK // HEAD_DIM
 CHUNKS_PER_STREAM = STREAM_COLS // CHUNK
 CHUNKS = 3 * CHUNKS_PER_STREAM
 Q, K, V = range(3)
+SCALE_TILES = 4
 
 FLOPS = 2 * BATCH * SEQ * DIM * 3 * STREAM_COLS
 
@@ -66,16 +67,17 @@ def tile_selfattention_pa_kernel(
             keep.tile([P, PASSES * P], U8, name="x_scales%d" % b, align_bytes=64)
             for b in range(BATCH)
         ]
-        loads = [(Q, 0, 1), (Q, 1, 1), (Q, 2, 2), (K, 0, 2), (V, 0, 2), (K, 2, 2), (V, 2, 2)]
+        loads = [(Q, 0, 1), (Q, 1, 1), (Q, 2, 2), (K, 0, 2), (K, 2, 2), (V, 0, 2), (V, 2, 2)]
         w_words = [
             keep.tile([P, PASSES, 2 * CHUNK * n], U8, name="w_words%d_%d" % (s, c), align_bytes=64)
             for s, c, n in loads
         ]
-        scale_loads = [(Q, 0, 2), (Q, 2, 2), (K, 0, 4), (V, 0, 4)]
-        w_scales = [
-            keep.tile([P, PASSES, CHUNK * n], U8, name="w_scales%d_%d" % (s, c), align_bytes=64)
-            for s, c, n in scale_loads
+        scale_loads = [(s, c, 2) for s in range(3) for c in (0, 2)]
+        scale_tiles = [
+            keep.tile([P, PASSES, 2 * CHUNK], U8, name="w_scales%d" % i, align_bytes=64)
+            for i in range(SCALE_TILES)
         ]
+        w_scales = [scale_tiles[j % SCALE_TILES] for j in range(len(scale_loads))]
         bias_rows = keep.tile([P, CHUNK], BF16, name="bias_rows")
         gain_rows = keep.tile([P, 2 * HEAD_DIM], BF16, name="gain_rows")
         bias_sb = keep.tile([P, 3 * STREAM_COLS], BF16, name="bias_sb")
@@ -108,8 +110,10 @@ def tile_selfattention_pa_kernel(
             )
         nc.scalar.activation(out=table_warm[:], in_=table_warm[:], func=ACT.Abs_reciprocal_sqrt)
 
-        for j in range(len(scale_loads)):
-            nc.vector.memset(w_scales[j][:].bitcast(I32), 0)
+        for i, tile in enumerate(scale_tiles):
+            nc.vector.memset(tile[:].bitcast(I32), 0)
+            if i == 0:
+                nc.vector.tensor_copy(out=ident_bf[:], in_=ident[:])
 
         def load_scale_planes(j):
             s, c, n = scale_loads[j]
@@ -143,8 +147,7 @@ def tile_selfattention_pa_kernel(
         load_scale_planes(2)
         load_words(3)
         load_scale_planes(3)
-        for j in range(4, len(loads)):
-            load_words(j)
+        load_words(4)
 
         def spread_row(out, rows, row):
             nc.tensor.matmul(
@@ -317,15 +320,7 @@ def tile_selfattention_pa_kernel(
                     scale=rrms[:, h : h + 1],
                 )
 
-        banks = [(Q, c, b) for c in range(CHUNKS_PER_STREAM) for b in range(BATCH)]
-        k_banks = [(K, c, b) for c in range(CHUNKS_PER_STREAM) for b in range(BATCH)]
-        v_banks = [(V, c, b) for c in range(CHUNKS_PER_STREAM) for b in range(BATCH)]
-        banks += k_banks[:2]
-        for k_bank, v_bank in zip(k_banks[2:], v_banks):
-            banks += [k_bank, v_bank]
-        banks += v_banks[-2:]
-
-        nc.vector.tensor_copy(out=ident_bf[:], in_=ident[:])
+        banks = [(Q, 0, 0), (Q, 0, 1), (Q, 1, 0), (Q, 1, 1), (Q, 2, 0), (Q, 2, 1), (Q, 3, 0), (Q, 3, 1), (K, 0, 0), (K, 0, 1), (K, 1, 0), (K, 1, 1), (V, 0, 0), (K, 2, 0), (V, 0, 1), (K, 2, 1), (V, 1, 0), (K, 3, 0), (V, 1, 1), (K, 3, 1), (V, 2, 0), (V, 2, 1), (V, 3, 0), (V, 3, 1)]
         transpose_x(0)
         make_tables()
         quantise_x(0)
@@ -341,6 +336,12 @@ def tile_selfattention_pa_kernel(
             if n < len(banks):
                 s, c, b = banks[n]
                 acc = project(s, c, b)
+                if (s, c, b) == (Q, 1, 1):
+                    load_scale_planes(4)
+                    load_words(5)
+                if (s, c, b) == (Q, 3, 1):
+                    load_scale_planes(5)
+                    load_words(6)
                 if n == 0:
                     place_tables(Q)
                 if n == 2:

@@ -67,7 +67,7 @@ def tile_selfattention_pa_kernel(
             keep.tile([P, PASSES * P], U8, name="x_scales%d" % b, align_bytes=64)
             for b in range(BATCH)
         ]
-        loads = [(Q, 0, 1), (Q, 1, 1), (Q, 2, 2), (K, 0, 2), (K, 2, 2), (V, 0, 2), (V, 2, 2)]
+        loads = [(Q, 0, 1), (Q, 1, 1), (Q, 2, 2), (K, 0, 4), (V, 0, 4)]
         w_words = [
             keep.tile([P, PASSES, 2 * CHUNK * n], U8, name="w_words%d_%d" % (s, c), align_bytes=64)
             for s, c, n in loads
@@ -147,7 +147,6 @@ def tile_selfattention_pa_kernel(
         load_scale_planes(2)
         load_words(3)
         load_scale_planes(3)
-        load_words(4)
 
         def spread_row(out, rows, row):
             nc.tensor.matmul(
@@ -338,10 +337,9 @@ def tile_selfattention_pa_kernel(
                 acc = project(s, c, b)
                 if (s, c, b) == (Q, 1, 1):
                     load_scale_planes(4)
-                    load_words(5)
+                    load_words(4)
                 if (s, c, b) == (Q, 3, 1):
                     load_scale_planes(5)
-                    load_words(6)
                 if n == 0:
                     place_tables(Q)
                 if n == 2:

@@ -328,10 +328,10 @@ def tile_selfattention_pa_kernel(
         turn_tables(Q)
         spread_bias(0)
 
-        to_rotate, to_normalise = [], []
+        to_rotate, to_normalise, to_bias = [], [], []
         for n in range(len(banks) + 2):
-            rotating, normalising = to_rotate, to_normalise
-            to_rotate, to_normalise = [], []
+            rotating, normalising, biasing = to_rotate, to_normalise, to_bias
+            to_rotate, to_normalise, to_bias = [], [], []
             if n < len(banks):
                 s, c, b = banks[n]
                 acc = project(s, c, b)
@@ -346,7 +346,11 @@ def tile_selfattention_pa_kernel(
                     turn_tables(K)
                 if n == 4:
                     place_tables(K)
-                if s == V:
+                if (s, c, b) in [(V, 0, 0), (V, 1, 0)]:
+                    v_sums = work.tile([P, CHUNK], F32, name="v_sums")
+                    nc.scalar.copy(out=v_sums[:], in_=acc[:])
+                    to_bias.append((c, b, v_sums))
+                elif s == V:
                     add_bias(s, c, acc, result_of(s, c)[:, :, b, :])
                     store(s, c, b)
                 else:
@@ -358,6 +362,17 @@ def tile_selfattention_pa_kernel(
             for s, c, b, u, sums in rotating:
                 rotated = add_products(multiply(s, b, u))
                 to_normalise.append((s, c, b, rotated, reciprocal_rms(sums)))
+            for c, b, v_sums in biasing:
+                first_col = V * STREAM_COLS + c * CHUNK
+                nc.gpsimd.tensor_tensor(
+                    out=result_of(V, c)[:, :, b, :],
+                    in0=v_sums[:].rearrange("p (h d) -> p h d", h=CHUNK_HEADS),
+                    in1=bias_sb[:, first_col : first_col + CHUNK].rearrange(
+                        "p (h d) -> p h d", h=CHUNK_HEADS
+                    ),
+                    op=ADD,
+                )
+                store(V, c, b)
             for s, c, b, rotated, rrms in normalising:
                 normalise(rotated, rrms, result_of(s, c)[:, :, b, :])
                 store(s, c, b)

@@ -162,21 +162,23 @@ def tile_selfattention_pa_kernel(
                 out=bias_sb[:, first * CHUNK : (first + 2) * CHUNK], in_=bank[:]
             )
 
-        def make_tables():
-            bank = psum.tile([P, 2 * HEAD_DIM], F32, tag="bank", name="gain_bank")
-            spread_row(bank[:], gain_rows, 0)
+        def spread_gains():
+            bank = coef[K][:].rearrange("p t j d -> p (t j d)")[:, : 2 * HEAD_DIM]
+            spread_row(bank, gain_rows, 0)
+            return bank
+
+        def make_table(gain_bank, s):
             pe_by_pair = pe_sb[:].rearrange("p t (i m) -> p t i m", m=4)
+            gain = gain_bank[:, s * HEAD_DIM : (s + 1) * HEAD_DIM]
             for j, taken in enumerate([slice(0, 4, 3), slice(2, 0, -1)]):
-                for s in range(2):
-                    gain = bank[:, s * HEAD_DIM : (s + 1) * HEAD_DIM]
-                    nc.vector.tensor_tensor(
-                        out=coef_sb[:, s, :, j, :].rearrange("p t (i e) -> p t i e", e=2),
-                        in0=pe_by_pair[:, :, :, taken],
-                        in1=gain.rearrange("p (i e) -> p i e", e=2)
-                        .unsqueeze(1)
-                        .to_broadcast([P, TOKEN_TILES, PAIRS, 2]),
-                        op=MULT,
-                    )
+                nc.vector.tensor_tensor(
+                    out=coef_sb[:, s, :, j, :].rearrange("p t (i e) -> p t i e", e=2),
+                    in0=pe_by_pair[:, :, :, taken],
+                    in1=gain.rearrange("p (i e) -> p i e", e=2)
+                    .unsqueeze(1)
+                    .to_broadcast([P, TOKEN_TILES, PAIRS, 2]),
+                    op=MULT,
+                )
 
         def turn_tables(s):
             bank = psum.tile([P, 4, P], F32, tag="bank", name="turned_bank")
@@ -321,7 +323,8 @@ def tile_selfattention_pa_kernel(
 
         banks = [(Q, 0, 0), (Q, 0, 1), (Q, 1, 0), (Q, 1, 1), (Q, 2, 0), (Q, 2, 1), (Q, 3, 0), (Q, 3, 1), (K, 0, 0), (K, 0, 1), (K, 1, 0), (K, 1, 1), (V, 0, 0), (K, 2, 0), (V, 0, 1), (K, 2, 1), (V, 1, 0), (K, 3, 0), (V, 1, 1), (K, 3, 1), (V, 2, 0), (V, 2, 1), (V, 3, 0), (V, 3, 1)]
         transpose_x(0)
-        make_tables()
+        gain_bank = spread_gains()
+        make_table(gain_bank, Q)
         quantise_x(0)
         transpose_x(1)
         quantise_x(1)
@@ -357,6 +360,8 @@ def tile_selfattention_pa_kernel(
                     u = work.tile([P, CHUNK], F32, name="u")
                     add_bias(s, c, acc, u[:].rearrange("p (h d) -> p h d", h=CHUNK_HEADS))
                     to_rotate.append((s, c, b, u, sum_squares(u)))
+                if n == 0:
+                    make_table(gain_bank, K)
                 if n % 2 == 1 and n < CHUNKS - 1:
                     spread_bias(n + 1)
             for s, c, b, u, sums in rotating:
@@ -375,4 +380,6 @@ def tile_selfattention_pa_kernel(
                 store(V, c, b)
             for s, c, b, rotated, rrms in normalising:
                 normalise(rotated, rrms, result_of(s, c)[:, :, b, :])
-                store(s, c, b)
+                if (s, c) != (K, CHUNKS_PER_STREAM - 1):
+                    store(s, c, b)
+        store(K, CHUNKS_PER_STREAM - 1, TOKEN_TILES - 1)

from contextlib import ExitStack

import concourse.masks as masks
import concourse.mybir as mybir

F32 = mybir.dt.float32
BF16 = mybir.dt.bfloat16
U8 = mybir.dt.uint8
U32 = mybir.dt.uint32
I32 = mybir.dt.int32
FP8X4 = mybir.dt.float8_e4m3fn_x4
FP4X4 = mybir.dt.float4_e2m1fn_x4
ADD = mybir.AluOpType.add
MULT = mybir.AluOpType.mult
ACT = mybir.ActivationFunctionType

P = 128
BATCH = 2
SEQ = 128
TOKEN_TILES = 2
DIM = 2048
HEADS = 16
HEAD_DIM = 128
PAIRS = HEAD_DIM // 2
EPS = 1e-6
K_PASS = 512
PASSES = DIM // K_PASS
STREAM_COLS = HEADS * HEAD_DIM
CHUNK = 512
CHUNK_HEADS = CHUNK // HEAD_DIM
CHUNKS_PER_STREAM = STREAM_COLS // CHUNK
CHUNKS = 3 * CHUNKS_PER_STREAM
Q, K, V = range(3)
SCALE_TILES = 4

FLOPS = 2 * BATCH * SEQ * DIM * 3 * STREAM_COLS


def tile_selfattention_pa_kernel(
    tc, x, pe, qkv_w_words, qkv_w_scales, qkv_b, q_scale, k_scale, out_0, out_1, out_2
):
    nc = tc.nc
    outs = [out_0, out_1, out_2]
    gains = [q_scale, k_scale]
    words_i32 = qkv_w_words.bitcast(I32)
    scales_i32 = qkv_w_scales.bitcast(I32)

    with ExitStack() as ctx:
        ctx.enter_context(tc.manual_schedule())
        keep = ctx.enter_context(tc.tile_pool(name="keep", bufs=1))
        work = ctx.enter_context(tc.tile_pool(name="work", bufs=6))
        stats = ctx.enter_context(tc.tile_pool(name="stats", bufs=6))
        results = ctx.enter_context(tc.tile_pool(name="results", bufs=CHUNKS))
        psum = ctx.enter_context(tc.psum_pool(name="psum", bufs=6))
        psum_keep = ctx.enter_context(tc.psum_pool(name="psum_keep", bufs=1))

        x_sb = [keep.tile([P, DIM], BF16, name="x_sb%d" % b) for b in range(TOKEN_TILES)]
        x_grouped = [
            keep.tile([P, PASSES * P * 4], BF16, name="x_grouped%d" % b, align_bytes=64)
            for b in range(BATCH)
        ]
        x_codes = [
            keep.tile([P, PASSES * P], U32, name="x_codes%d" % b, align_bytes=64)
            for b in range(BATCH)
        ]
        x_scales = [
            keep.tile([P, PASSES * P], U8, name="x_scales%d" % b, align_bytes=64)
            for b in range(BATCH)
        ]
        loads = [(Q, 0, 1), (Q, 1, 1), (Q, 2, 2), (K, 0, 4), (V, 0, 4)]
        w_words = [
            keep.tile([P, PASSES, 2 * CHUNK * n], U8, name="w_words%d_%d" % (s, c), align_bytes=64)
            for s, c, n in loads
        ]
        scale_loads = [(s, c, 2) for s in range(3) for c in (0, 2)]
        scale_tiles = [
            keep.tile([P, PASSES, 2 * CHUNK], U8, name="w_scales%d" % i, align_bytes=64)
            for i in range(SCALE_TILES)
        ]
        w_scales = [scale_tiles[j % SCALE_TILES] for j in range(len(scale_loads))]
        bias_rows = keep.tile([P, CHUNK], BF16, name="bias_rows")
        gain_rows = keep.tile([P, 2 * HEAD_DIM], BF16, name="gain_rows")
        bias_sb = keep.tile([P, 3 * STREAM_COLS], BF16, name="bias_sb")
        pe_sb = keep.tile([P, TOKEN_TILES, 4 * PAIRS], BF16, name="pe_sb")
        coef_sb = keep.tile([P, 2, TOKEN_TILES, 2, HEAD_DIM], F32, name="coef_sb")
        coef_turned = [keep.tile([P, 4, P], F32, name="coef_turned%d" % s) for s in range(2)]
        coef = [
            psum_keep.tile([P, TOKEN_TILES, 2, HEAD_DIM], F32, name="coef%d" % s) for s in range(2)
        ]
        ident = keep.tile([P, P], F32, name="ident")
        ident_bf = keep.tile([P, P], BF16, name="ident_bf")
        table_warm = keep.tile([P, 1], F32, name="table_warm")

        nc.vector.memset(bias_rows[:].bitcast(I32), 0)
        nc.vector.memset(gain_rows[:].bitcast(I32), 0)
        nc.vector.memset(table_warm[:], 1.0)
        nc.scalar.dma_start(
            out=bias_rows[0:CHUNKS, :], in_=qkv_b.rearrange("(c n) -> c n", n=CHUNK)
        )
        masks.make_identity(nc, ident[:])
        for s in range(2):
            nc.scalar.dma_start(
                out=gain_rows[0:1, s * HEAD_DIM : (s + 1) * HEAD_DIM],
                in_=gains[s].rearrange("(o n) -> o n", o=1),
            )
        for b in range(BATCH):
            nc.scalar.dma_start(
                out=pe_sb[b:P:BATCH].rearrange("p t m -> p (t m)"),
                in_=pe.rearrange("a b (j t) i e f -> (a b j) (t i e f)", t=TOKEN_TILES),
            )
        nc.scalar.activation(out=table_warm[:], in_=table_warm[:], func=ACT.Abs_reciprocal_sqrt)

        for i, tile in enumerate(scale_tiles):
            nc.vector.memset(tile[:].bitcast(I32), 0)
            if i == 0:
                nc.vector.tensor_copy(out=ident_bf[:], in_=ident[:])

        def load_scale_planes(j):
            s, c, n = scale_loads[j]
            first = (s * CHUNKS_PER_STREAM + c) * CHUNK // 4
            cols = slice(first, first + n * CHUNK // 4)
            for r in range(4):
                nc.sync.dma_start(
                    out=w_scales[j][r : P : 32].bitcast(I32),
                    in_=scales_i32[:, r : 16 : 4, cols].rearrange("g q n -> q g n"),
                )

        def load_words(j):
            s, c, n = loads[j]
            first = (s * CHUNKS_PER_STREAM + c) * CHUNK // 2
            nc.sync.dma_start(
                out=w_words[j][:].bitcast(I32),
                in_=words_i32[:, :, first : first + n * CHUNK // 2].rearrange("g p c -> p g c"),
            )

        for t in range(TOKEN_TILES):
            for b in range(BATCH):
                nc.sync.dma_start(
                    out=x_sb[t][b:P:BATCH],
                    in_=x[b].rearrange("(j t) k -> t j k", t=TOKEN_TILES)[t],
                )
        load_scale_planes(0)
        load_words(0)
        load_words(1)
        load_scale_planes(1)
        load_words(2)
        load_scale_planes(2)
        load_words(3)
        load_scale_planes(3)

        def spread_row(out, rows, row):
            nc.tensor.matmul(
                out=out, lhsT=ident_bf[:, row : row + 1].to_broadcast([P, P]), rhs=rows[:],
                start=True, stop=True,
            )

        def spread_bias(first):
            bank = psum.tile([P, 2 * CHUNK], BF16, tag="bank", name="bias_bank")
            for i in range(2):
                spread_row(bank[:, i * CHUNK : (i + 1) * CHUNK], bias_rows, first + i)
            nc.scalar.copy(
                out=bias_sb[:, first * CHUNK : (first + 2) * CHUNK], in_=bank[:]
            )

        def spread_gains():
            bank = coef[K][:].rearrange("p t j d -> p (t j d)")[:, : 2 * HEAD_DIM]
            spread_row(bank, gain_rows, 0)
            return bank

        def make_table(gain_bank, s):
            pe_by_pair = pe_sb[:].rearrange("p t (i m) -> p t i m", m=4)
            gain = gain_bank[:, s * HEAD_DIM : (s + 1) * HEAD_DIM]
            for j, taken in enumerate([slice(0, 4, 3), slice(2, 0, -1)]):
                nc.vector.tensor_tensor(
                    out=coef_sb[:, s, :, j, :].rearrange("p t (i e) -> p t i e", e=2),
                    in0=pe_by_pair[:, :, :, taken],
                    in1=gain.rearrange("p (i e) -> p i e", e=2)
                    .unsqueeze(1)
                    .to_broadcast([P, TOKEN_TILES, PAIRS, 2]),
                    op=MULT,
                )

        def turn_tables(s):
            bank = psum.tile([P, 4, P], F32, tag="bank", name="turned_bank")
            tables = coef_sb[:, s].rearrange("p t j d -> p (t j) d")
            for i in range(4):
                nc.tensor.transpose(out=bank[:, i, :], in_=tables[:, i, :], identity=ident[:])
            nc.scalar.copy(out=coef_turned[s][:], in_=bank[:])

        def place_tables(s):
            tables = coef[s][:].rearrange("p t j d -> p (t j) d")
            for i in range(4):
                nc.tensor.transpose(
                    out=tables[:, i, :], in_=coef_turned[s][:, i, :], identity=ident[:]
                )

        def transpose_x(b):
            words = x_sb[b][:].bitcast(F32)
            grouped = x_grouped[b][:].bitcast(F32).rearrange(
                "p (g r u) -> p g r u", g=PASSES, u=2
            )
            for half in range(PASSES // 2):
                xt = psum.tile([P, 4, P], F32, tag="bank", name="xt")
                for gg in range(2):
                    g = 2 * half + gg
                    for u in range(2):
                        nc.tensor.transpose(
                            out=xt[:, 2 * gg + u, :],
                            in_=words[:, 256 * g + u : 256 * (g + 1) : 2],
                            identity=ident[:],
                        )
                source = xt[:].rearrange("p (gg u) r -> p gg r u", u=2)
                target = grouped[:, 2 * half : 2 * half + 2]
                if half == 0:
                    nc.vector.tensor_copy(out=target, in_=source)
                else:
                    nc.scalar.copy(out=target, in_=source)

        def quantise_x(b):
            nc.vector.quantize_mx(
                out=x_codes[b][:].bitcast(FP8X4), scales=x_scales[b][:], in_=x_grouped[b][:]
            )

        def find_load(table, s, c):
            for j, (ls, first, n) in enumerate(table):
                if ls == s and first <= c < first + n:
                    return j, c - first

        def project(s, c, b):
            j, part = find_load(loads, s, c)
            sj, spart = find_load(scale_loads, s, c)
            acc = psum.tile([P, CHUNK], F32, tag="bank", name="acc")
            for g in range(PASSES):
                tokens = slice(g * P, (g + 1) * P)
                nc.tensor.matmul_mx(
                    out=acc[:],
                    lhsT=x_codes[b][:, tokens].bitcast(FP8X4),
                    lhsT_scale=x_scales[b][:, tokens],
                    rhs=w_words[j][:, g, 2 * CHUNK * part : 2 * CHUNK * (part + 1)].bitcast(FP4X4),
                    rhs_scale=w_scales[sj][:, g, CHUNK * spart : CHUNK * (spart + 1)],
                    start=(g == 0),
                    stop=(g == PASSES - 1),
                )
            return acc

        chunk_results = {}

        def result_of(s, c):
            if (s, c) not in chunk_results:
                chunk_results[s, c] = results.tile(
                    [P, CHUNK_HEADS, TOKEN_TILES, HEAD_DIM], F32, name="res"
                )
            return chunk_results[s, c]

        def store(s, c, t):
            if t == 0:
                return
            heads = slice(c * CHUNK_HEADS, (c + 1) * CHUNK_HEADS)
            res = result_of(s, c)
            for b in range(BATCH):
                nc.sync.dma_start(
                    out=outs[s][b, heads].rearrange("h (j t) d -> j h (t d)", t=TOKEN_TILES),
                    in_=res[b:P:BATCH].rearrange("p h t d -> p h (t d)"),
                )

        def add_bias(s, c, acc, out):
            first_col = s * STREAM_COLS + c * CHUNK
            bias = bias_sb[:, first_col : first_col + CHUNK]
            nc.vector.tensor_tensor(
                out=out,
                in0=acc[:].rearrange("p (h d) -> p h d", h=CHUNK_HEADS),
                in1=bias.rearrange("p (h d) -> p h d", h=CHUNK_HEADS),
                op=ADD,
            )

        def sum_squares(u):
            squares = work.tile([P, CHUNK], F32, name="squares")
            sums = stats.tile([P, CHUNK_HEADS], F32, name="sums")
            for h in range(CHUNK_HEADS):
                head = slice(h * HEAD_DIM, (h + 1) * HEAD_DIM)
                nc.scalar.activation(
                    out=squares[:, head], in_=u[:, head], func=ACT.Square,
                    accum_out=sums[:, h : h + 1],
                )
            return sums

        def reciprocal_rms(sums):
            rrms = stats.tile([P, CHUNK_HEADS], F32, name="rrms")
            nc.scalar.activation(
                out=rrms[:], in_=sums[:], func=ACT.Abs_reciprocal_sqrt,
                scale=1.0 / HEAD_DIM, bias=EPS,
            )
            return rrms

        def multiply(s, t, u):
            products = work.tile([P, 2, CHUNK], F32, name="products")
            shape = [P, 2, CHUNK_HEADS, HEAD_DIM]
            nc.vector.tensor_tensor(
                out=products[:].rearrange("p j (h d) -> p j h d", h=CHUNK_HEADS),
                in0=u[:].rearrange("p (h d) -> p h d", h=CHUNK_HEADS).unsqueeze(1).to_broadcast(shape),
                in1=coef[s][:, t].unsqueeze(2).to_broadcast(shape),
                op=MULT,
            )
            return products

        def add_products(products):
            rotated = work.tile([P, CHUNK], F32, name="rotated")
            nc.gpsimd.tensor_tensor(
                out=rotated[:].rearrange("p (c e) -> p c e", e=2),
                in0=products[:, 0, :].rearrange("p (c e) -> p c e", e=2),
                in1=products[:, 1, :].rearrange("p (c e) -> p c e", e=2)[:, :, ::-1],
                op=ADD,
            )
            return rotated

        def normalise(rotated, rrms, out):
            for h in range(CHUNK_HEADS):
                head = slice(h * HEAD_DIM, (h + 1) * HEAD_DIM)
                nc.scalar.activation(
                    out=out[:, h, :], in_=rotated[:, head], func=ACT.Copy,
                    scale=rrms[:, h : h + 1],
                )

        banks = [(Q, 0, 0), (Q, 0, 1), (Q, 1, 0), (Q, 1, 1), (Q, 2, 0), (Q, 2, 1), (Q, 3, 0), (Q, 3, 1), (K, 0, 0), (K, 0, 1), (K, 1, 0), (K, 1, 1), (V, 0, 0), (K, 2, 0), (V, 0, 1), (K, 2, 1), (V, 1, 0), (K, 3, 0), (V, 1, 1), (K, 3, 1), (V, 2, 0), (V, 2, 1), (V, 3, 0), (V, 3, 1)]
        transpose_x(0)
        gain_bank = spread_gains()
        make_table(gain_bank, Q)
        quantise_x(0)
        transpose_x(1)
        quantise_x(1)
        turn_tables(Q)
        spread_bias(0)

        to_rotate, to_normalise, to_bias = [], [], []
        for n in range(len(banks) + 2):
            rotating, normalising, biasing = to_rotate, to_normalise, to_bias
            to_rotate, to_normalise, to_bias = [], [], []
            if n < len(banks):
                s, c, b = banks[n]
                acc = project(s, c, b)
                if (s, c, b) == (Q, 1, 1):
                    load_scale_planes(4)
                    load_words(4)
                if (s, c, b) == (Q, 3, 1):
                    load_scale_planes(5)
                if n == 0:
                    place_tables(Q)
                if n == 2:
                    turn_tables(K)
                if n == 4:
                    place_tables(K)
                if (s, c, b) in [(V, 0, 0), (V, 1, 0)]:
                    v_sums = work.tile([P, CHUNK], F32, name="v_sums")
                    nc.scalar.copy(out=v_sums[:], in_=acc[:])
                    to_bias.append((c, b, v_sums))
                elif s == V:
                    add_bias(s, c, acc, result_of(s, c)[:, :, b, :])
                    store(s, c, b)
                else:
                    u = work.tile([P, CHUNK], F32, name="u")
                    add_bias(s, c, acc, u[:].rearrange("p (h d) -> p h d", h=CHUNK_HEADS))
                    to_rotate.append((s, c, b, u, sum_squares(u)))
                if n == 0:
                    make_table(gain_bank, K)
                if n % 2 == 1 and n < CHUNKS - 1:
                    spread_bias(n + 1)
            for s, c, b, u, sums in rotating:
                rotated = add_products(multiply(s, b, u))
                to_normalise.append((s, c, b, rotated, reciprocal_rms(sums)))
            for c, b, v_sums in biasing:
                first_col = V * STREAM_COLS + c * CHUNK
                nc.gpsimd.tensor_tensor(
                    out=result_of(V, c)[:, :, b, :],
                    in0=v_sums[:].rearrange("p (h d) -> p h d", h=CHUNK_HEADS),
                    in1=bias_sb[:, first_col : first_col + CHUNK].rearrange(
                        "p (h d) -> p h d", h=CHUNK_HEADS
                    ),
                    op=ADD,
                )
                store(V, c, b)
            for s, c, b, rotated, rrms in normalising:
                normalise(rotated, rrms, result_of(s, c)[:, :, b, :])
                if (s, c) != (K, CHUNKS_PER_STREAM - 1):
                    store(s, c, b)
        store(K, CHUNKS_PER_STREAM - 1, TOKEN_TILES - 1)
